import numpy as np
import ml_dtypes

BF16 = ml_dtypes.bfloat16


def bf(x):
    return np.asarray(x, np.float32).astype(BF16)


def f32(x):
    return np.asarray(x, np.float32)


def f64(x):
    return np.asarray(x).astype(np.float64)


def striped(idx):
    return np.tile(idx.reshape(-1, 16).T, (8, 1))


V, D, N = 512, 128, 1024


def relu(v):
    return np.maximum(v, 0.0)


def setup_inputs():
    return {"table": bf(np.random.standard_normal((D, V))), "w1": bf(np.random.standard_normal((D, D)) / np.sqrt(D)), "w2": bf(np.random.standard_normal((D, D)) / np.sqrt(D)), "w3": bf(np.random.standard_normal((D, D)) / np.sqrt(D)), "offs": striped(np.random.permutation(np.tile(np.arange(V), 2))[:N])}


def reference(table, w1, w2, w3, offs):
    idx = offs[:16].T.reshape(-1)
    h1 = relu(f64(w1).T @ f64(table)[:, idx])
    h2 = relu(f64(w2).T @ h1)
    return relu(f64(w3).T @ h2)

@@ -1,0 +1,74 @@
+import concourse.mybir as mybir
+
+BF16, F32, U16 = mybir.dt.bfloat16, mybir.dt.float32, mybir.dt.uint16
+RELU = mybir.ActivationFunctionType.Relu
+
+P = 128
+TYPES = 512
+ATOMS = 1024
+WIDTHS = (128, 256, 256, 256, 128)
+STARTS = tuple(sum(WIDTHS[:piece]) for piece in range(len(WIDTHS)))
+N_PIECES = len(WIDTHS)
+assert sum(WIDTHS) == ATOMS and all(width % 32 == 0 for width in WIDTHS)
+BANK = 512
+PSUM_BANKS = 8
+WARM_MATMULS = 3
+
+FLOPS = 3 * 2 * P * P * ATOMS
+
+
+def relu_from_psum(nc, piece, dst, src):
+    if piece % 2 == 0:
+        nc.vector.tensor_scalar_max(dst, src, 0.0)
+    else:
+        nc.scalar.activation(dst, src, RELU)
+
+
+def tile_gcn_1_kernel(tc, table, w1, w2, w3, offs, out):
+    nc = tc.nc
+    with (
+        tc.tile_pool(name="held", bufs=1) as held,
+        tc.tile_pool(name="acts", bufs=N_PIECES) as acts,
+        tc.psum_pool(name="idle", bufs=1) as idle,
+        tc.psum_pool(name="psum", bufs=PSUM_BANKS - 1) as psum,
+    ):
+        zeros = held.tile([P, BANK], BF16, name="zeros")
+        nc.vector.memset(zeros[:], 0.0)
+        unread = idle.tile([P, BANK], F32, name="unread")
+        for warm in range(WARM_MATMULS):
+            nc.tensor.matmul(unread[:], zeros[:, :P], zeros[:], start=True, stop=True)
+
+        offsets = held.tile([P, ATOMS // 16], U16, name="offsets")
+        nc.sync.dma_start(offsets[:], offs)
+        table_sb = held.tile([P, TYPES], BF16, name="table_sb")
+        nc.scalar.dma_start(table_sb[:], table)
+        w1_sb = held.tile([P, P], BF16, name="w1_sb")
+        nc.sync.dma_start(w1_sb[:], w1)
+        w2_sb = held.tile([P, P], BF16, name="w2_sb")
+        nc.scalar.dma_start(w2_sb[:], w2)
+        w3_sb = held.tile([P, P], BF16, name="w3_sb")
+        nc.sync.dma_start(w3_sb[:], w3)
+
+        h1 = []
+        for piece, (start, width) in enumerate(zip(STARTS, WIDTHS)):
+            picked = table_sb[:].indirect(offsets[:, start // 16 : (start + width) // 16])
+            sums = psum.tile([P, width], F32, name="sums")
+            nc.tensor.matmul(sums[:], w1_sb[:], picked, start=True, stop=True)
+            hidden = acts.tile([P, width], BF16, name="h1")
+            relu_from_psum(nc, piece, hidden[:], sums[:])
+            h1.append(hidden)
+
+        h2 = []
+        for piece, width in enumerate(WIDTHS):
+            sums = psum.tile([P, width], BF16, name="sums")
+            nc.tensor.matmul(sums[:], w2_sb[:], h1[piece][:], start=True, stop=True)
+            hidden = acts.tile([P, width], BF16, name="h2")
+            nc.vector.tensor_scalar_max(hidden[:], sums[:], 0.0)
+            h2.append(hidden)
+
+        for piece, (start, width) in enumerate(zip(STARTS, WIDTHS)):
+            sums = psum.tile([P, width], F32, name="sums")
+            nc.tensor.matmul(sums[:], w3_sb[:], h2[piece][:], start=True, stop=True)
+            result = acts.tile([P, width], F32, name="result")
+            relu_from_psum(nc, piece, result[:], sums[:])
+            nc.sync.dma_start(out[:, start : start + width], result[:])

@@ -66,9 +66,12 @@ def tile_gcn_1_kernel(tc, table, w1, w2, w3, offs, out):
             nc.vector.tensor_scalar_max(hidden[:], sums[:], 0.0)
             h2.append(hidden)
 
+        result = held.tile([P, ATOMS], F32, name="result")
         for piece, (start, width) in enumerate(zip(STARTS, WIDTHS)):
             sums = psum.tile([P, width], F32, name="sums")
             nc.tensor.matmul(sums[:], w3_sb[:], h2[piece][:], start=True, stop=True)
-            result = acts.tile([P, width], F32, name="result")
-            relu_from_psum(nc, piece, result[:], sums[:])
-            nc.sync.dma_start(out[:, start : start + width], result[:])
+            end = start + width
+            relu_from_psum(nc, piece, result[:, start:end], sums[:])
+            if piece % 2 or piece == N_PIECES - 1:
+                first = STARTS[piece - piece % 2]
+                nc.sync.dma_start(out[:, first:end], result[:, first:end])

@@ -10,6 +10,7 @@ WIDTHS = (128, 256, 256, 256, 128)
 STARTS = tuple(sum(WIDTHS[:piece]) for piece in range(len(WIDTHS)))
 N_PIECES = len(WIDTHS)
 assert sum(WIDTHS) == ATOMS and all(width % 32 == 0 for width in WIDTHS)
+STORE_BEHIND = (1, 2, 4)
 BANK = 512
 PSUM_BANKS = 8
 WARM_MATMULS = 3
@@ -67,11 +68,12 @@ def tile_gcn_1_kernel(tc, table, w1, w2, w3, offs, out):
             h2.append(hidden)
 
         result = held.tile([P, ATOMS], F32, name="result")
+        stored = 0
         for piece, (start, width) in enumerate(zip(STARTS, WIDTHS)):
             sums = psum.tile([P, width], F32, name="sums")
             nc.tensor.matmul(sums[:], w3_sb[:], h2[piece][:], start=True, stop=True)
             end = start + width
             relu_from_psum(nc, piece, result[:, start:end], sums[:])
-            if piece % 2 or piece == N_PIECES - 1:
-                first = STARTS[piece - piece % 2]
-                nc.sync.dma_start(out[:, first:end], result[:, first:end])
+            if piece in STORE_BEHIND:
+                nc.sync.dma_start(out[:, stored:end], result[:, stored:end])
+                stored = end

@@ -6,11 +6,11 @@ RELU = mybir.ActivationFunctionType.Relu
 P = 128
 TYPES = 512
 ATOMS = 1024
-WIDTHS = (128, 256, 256, 256, 128)
+WIDTHS = (192, 192, 192, 192, 128, 128)
 STARTS = tuple(sum(WIDTHS[:piece]) for piece in range(len(WIDTHS)))
 N_PIECES = len(WIDTHS)
 assert sum(WIDTHS) == ATOMS and all(width % 32 == 0 for width in WIDTHS)
-STORE_BEHIND = (1, 2, 4)
+STORE_BEHIND = (1, 3, 5)
 BANK = 512
 PSUM_BANKS = 8
 WARM_MATMULS = 3
@@ -19,7 +19,7 @@ FLOPS = 3 * 2 * P * P * ATOMS
 
 
 def relu_from_psum(nc, piece, dst, src):
-    if piece % 2 == 0:
+    if piece % 2 == 1:
         nc.vector.tensor_scalar_max(dst, src, 0.0)
     else:
         nc.scalar.activation(dst, src, RELU)

@@ -6,11 +6,11 @@ RELU = mybir.ActivationFunctionType.Relu
 P = 128
 TYPES = 512
 ATOMS = 1024
-WIDTHS = (192, 192, 192, 192, 128, 128)
+WIDTHS = (160, 192, 192, 192, 160, 128)
 STARTS = tuple(sum(WIDTHS[:piece]) for piece in range(len(WIDTHS)))
 N_PIECES = len(WIDTHS)
 assert sum(WIDTHS) == ATOMS and all(width % 32 == 0 for width in WIDTHS)
-STORE_BEHIND = (1, 3, 5)
+STORE_BEHIND = (0, 2, 5)
 BANK = 512
 PSUM_BANKS = 8
 WARM_MATMULS = 3

@@ -6,11 +6,11 @@ RELU = mybir.ActivationFunctionType.Relu
 P = 128
 TYPES = 512
 ATOMS = 1024
-WIDTHS = (160, 192, 192, 192, 160, 128)
+WIDTHS = (128, 128, 256, 192, 192, 128)
 STARTS = tuple(sum(WIDTHS[:piece]) for piece in range(len(WIDTHS)))
 N_PIECES = len(WIDTHS)
 assert sum(WIDTHS) == ATOMS and all(width % 32 == 0 for width in WIDTHS)
-STORE_BEHIND = (0, 2, 5)
+STORE_BEHIND = (1, 2, 5)
 BANK = 512
 PSUM_BANKS = 8
 WARM_MATMULS = 3

import concourse.mybir as mybir

BF16, F32, U16 = mybir.dt.bfloat16, mybir.dt.float32, mybir.dt.uint16
RELU = mybir.ActivationFunctionType.Relu

P = 128
TYPES = 512
ATOMS = 1024
WIDTHS = (128, 128, 256, 192, 192, 128)
STARTS = tuple(sum(WIDTHS[:piece]) for piece in range(len(WIDTHS)))
N_PIECES = len(WIDTHS)
assert sum(WIDTHS) == ATOMS and all(width % 32 == 0 for width in WIDTHS)
STORE_BEHIND = (1, 2, 5)
BANK = 512
PSUM_BANKS = 8
WARM_MATMULS = 3

FLOPS = 3 * 2 * P * P * ATOMS


def relu_from_psum(nc, piece, dst, src):
    if piece % 2 == 1:
        nc.vector.tensor_scalar_max(dst, src, 0.0)
    else:
        nc.scalar.activation(dst, src, RELU)


def tile_gcn_1_kernel(tc, table, w1, w2, w3, offs, out):
    nc = tc.nc
    with (
        tc.tile_pool(name="held", bufs=1) as held,
        tc.tile_pool(name="acts", bufs=N_PIECES) as acts,
        tc.psum_pool(name="idle", bufs=1) as idle,
        tc.psum_pool(name="psum", bufs=PSUM_BANKS - 1) as psum,
    ):
        zeros = held.tile([P, BANK], BF16, name="zeros")
        nc.vector.memset(zeros[:], 0.0)
        unread = idle.tile([P, BANK], F32, name="unread")
        for warm in range(WARM_MATMULS):
            nc.tensor.matmul(unread[:], zeros[:, :P], zeros[:], start=True, stop=True)

        offsets = held.tile([P, ATOMS // 16], U16, name="offsets")
        nc.sync.dma_start(offsets[:], offs)
        table_sb = held.tile([P, TYPES], BF16, name="table_sb")
        nc.scalar.dma_start(table_sb[:], table)
        w1_sb = held.tile([P, P], BF16, name="w1_sb")
        nc.sync.dma_start(w1_sb[:], w1)
        w2_sb = held.tile([P, P], BF16, name="w2_sb")
        nc.scalar.dma_start(w2_sb[:], w2)
        w3_sb = held.tile([P, P], BF16, name="w3_sb")
        nc.sync.dma_start(w3_sb[:], w3)

        h1 = []
        for piece, (start, width) in enumerate(zip(STARTS, WIDTHS)):
            picked = table_sb[:].indirect(offsets[:, start // 16 : (start + width) // 16])
            sums = psum.tile([P, width], F32, name="sums")
            nc.tensor.matmul(sums[:], w1_sb[:], picked, start=True, stop=True)
            hidden = acts.tile([P, width], BF16, name="h1")
            relu_from_psum(nc, piece, hidden[:], sums[:])
            h1.append(hidden)

        h2 = []
        for piece, width in enumerate(WIDTHS):
            sums = psum.tile([P, width], BF16, name="sums")
            nc.tensor.matmul(sums[:], w2_sb[:], h1[piece][:], start=True, stop=True)
            hidden = acts.tile([P, width], BF16, name="h2")
            nc.vector.tensor_scalar_max(hidden[:], sums[:], 0.0)
            h2.append(hidden)

        result = held.tile([P, ATOMS], F32, name="result")
        stored = 0
        for piece, (start, width) in enumerate(zip(STARTS, WIDTHS)):
            sums = psum.tile([P, width], F32, name="sums")
            nc.tensor.matmul(sums[:], w3_sb[:], h2[piece][:], start=True, stop=True)
            end = start + width
            relu_from_psum(nc, piece, result[:, start:end], sums[:])
            if piece in STORE_BEHIND:
                nc.sync.dma_start(out[:, stored:end], result[:, stored:end])
                stored = end
